import numpy as np
import ml_dtypes


def mxq(x, axis, fmt="e4m3"):
    dtype, down = {"e4m3": (ml_dtypes.float8_e4m3fn, 7), "e5m2": (ml_dtypes.float8_e5m2, 14)}[fmt]
    v = np.moveaxis(np.asarray(x, np.float32).astype(ml_dtypes.bfloat16).astype(np.float64), axis, -1)
    blocks = v.reshape(v.shape[:-1] + (-1, 32))
    amax = np.abs(blocks).max(-1, keepdims=True)
    byte = np.maximum(np.where(amax > 0, np.frexp(amax)[1] - 1 + 127, 0) - down, 1)
    scale = np.exp2(byte - 127.0)
    codes = (blocks / scale).astype(np.float32).astype(dtype).astype(np.float64)
    return np.moveaxis((codes * scale).reshape(v.shape), -1, axis)


WIDE = False


def mx_kscale(k):
    if not WIDE:
        return np.ones(k)
    levels = np.array([10, -10, 5, -5, 0])
    if k % 512:
        return np.exp2(np.random.permutation(np.resize(levels, k // 32))).repeat(32)
    a = np.empty((k // 512, 16))
    for p in range(k // 512):
        a[p, :8] = np.random.permutation(np.resize(levels, 8))
        for g in range(8):
            far = levels[np.abs(levels - a[p, g]) >= 10]
            a[p, g + 8] = far[np.random.randint(len(far))]
    return np.exp2(a.ravel()).repeat(32)


BF16 = ml_dtypes.bfloat16


def bf(x):
    return np.asarray(x, np.float32).astype(BF16)


def f64(x):
    return np.asarray(x).astype(np.float64)


N, F, K, D, E = 512, 2048, 1536, 1024, 1024
SIG = 2.0
PS = 16.0


def setup_inputs():
    t, sx = mx_kscale(K), mx_kscale(F)
    s = np.concatenate([sx, np.ones(E)])
    g = SIG * np.random.standard_normal((N, K))
    e = np.exp(g - g.max(-1, keepdims=True))
    w = e / e.sum(-1, keepdims=True) * (np.random.uniform(size=K) * PS)[None, :]
    return {"att_prior": bf(w * t[None, :]),
            "dic": bf(np.random.standard_normal((K, D)) / t[:, None]),
            "x": bf(np.random.standard_normal((N, F)) * sx[None, :]),
            "cs_w": bf(np.random.standard_normal((K, F + E)) * (F + E) ** -0.5 / s[None, :]),
            "cs_b": bf(np.random.standard_normal(K) * 0.1)}


def reference(att_prior, dic, x, cs_w, cs_b):
    z = mxq(f64(att_prior), 1, "e4m3") @ mxq(f64(dic), 0, "e4m3")
    xz = np.concatenate([f64(x), z], axis=1)
    causal_logits = (mxq(xz, 1, "e4m3") @ mxq(f64(cs_w), 1, "e4m3").T) + f64(cs_b)
    return causal_logits, z

@@ -1,0 +1,237 @@
+from contextlib import ExitStack
+
+import concourse.mybir as mybir
+from concourse.masks import make_identity
+
+F32 = mybir.dt.float32
+BF16 = mybir.dt.bfloat16
+U32 = mybir.dt.uint32
+U8 = mybir.dt.uint8
+FP8X4 = mybir.dt.float8_e4m3fn_x4
+
+P = 128
+PACK = 4
+K_PASS = P * PACK
+ROWS = 512
+ROW_TILES = ROWS // P
+
+TOKENS, DICT, Z_DIM, X_DIM, OUT_DIM = 512, 1536, 1024, 2048, 1536
+XZ_DIM = X_DIM + Z_DIM
+DICT_PASSES = DICT // K_PASS
+X_PASSES = X_DIM // K_PASS
+Z_PASSES = Z_DIM // K_PASS
+XZ_PASSES = XZ_DIM // K_PASS
+
+RUN_PASSES = 2
+LOAD_K = RUN_PASSES * K_PASS
+RUNS_PER_CHUNK = XZ_PASSES // RUN_PASSES
+CHUNKS = OUT_DIM // ROWS
+W_RUNS = CHUNKS * RUNS_PER_CHUNK
+X_RUNS = X_PASSES // RUN_PASSES
+AHEAD = 2
+
+FIRST_LOADS = 13
+FIRST_W_LOADS = FIRST_LOADS - 7
+
+FLOPS = 2 * TOKENS * DICT * Z_DIM + 2 * TOKENS * XZ_DIM * OUT_DIM
+
+
+def tile_visualdeconfounder_pb_kernel(tc, att_prior, dic, x, cs_w, cs_b, out_0, out_1):
+    nc = tc.nc
+    logits_out, z_out = out_0, out_1
+
+    with ExitStack() as ctx:
+        const = ctx.enter_context(tc.tile_pool(name="const", bufs=1))
+        keep = ctx.enter_context(tc.tile_pool(name="keep", bufs=1))
+        raw_pool = ctx.enter_context(tc.tile_pool(name="raw", bufs=FIRST_LOADS))
+        grouped_pool = ctx.enter_context(tc.tile_pool(name="grouped", bufs=6))
+        chunk_pool = ctx.enter_context(tc.tile_pool(name="chunk", bufs=2))
+        result_pool = ctx.enter_context(tc.tile_pool(name="result", bufs=4))
+        transposed = ctx.enter_context(tc.psum_pool(name="transposed", bufs=4))
+        sums = ctx.enter_context(tc.psum_pool(name="sums", bufs=4))
+        ctx.enter_context(tc.manual_schedule())
+
+        def load_k_last(matrix, row0, k0, width):
+            raw = raw_pool.tile([P, ROW_TILES, LOAD_K], BF16, tag="raw")
+            nc.sync.dma_start(
+                out=raw[:, :, 0:width],
+                in_=matrix[row0 : row0 + ROWS, k0 : k0 + width].rearrange("(t p) k -> p t k", p=P),
+            )
+            return raw
+
+        def load_dic(c):
+            raw = raw_pool.tile([P, PACK, Z_DIM], BF16, tag="raw")
+            nc.sync.dma_start(
+                out=raw[:],
+                in_=dic[c * K_PASS : (c + 1) * K_PASS, :].rearrange("(p t) d -> p t d", t=PACK),
+            )
+            return raw
+
+        def load_w(j):
+            chunk, r = divmod(j, RUNS_PER_CHUNK)
+            return load_k_last(cs_w, chunk * ROWS, r * LOAD_K, LOAD_K)
+
+        att_raw = [load_k_last(att_prior, 0, 0, LOAD_K), load_k_last(att_prior, 0, LOAD_K, DICT - LOAD_K)]
+        dic_raw = [load_dic(c) for c in range(DICT_PASSES)]
+        x_raw = [load_k_last(x, 0, r * LOAD_K, LOAD_K) for r in range(X_DIM // LOAD_K)]
+        w_raw = [load_w(j) for j in range(FIRST_W_LOADS)]
+        bias = const.tile([P, OUT_DIM], BF16)
+        nc.sync.dma_start(out=bias[:], in_=cs_b.partition_broadcast(P))
+
+        identity = const.tile([P, P], F32)
+        make_identity(nc, identity[:])
+
+        att_codes = keep.tile([P, DICT_PASSES, TOKENS], U32, align_bytes=64)
+        att_scales = keep.tile([P, DICT_PASSES, TOKENS], U8, align_bytes=64)
+        dic_codes = keep.tile([P, DICT_PASSES, Z_DIM], U32, align_bytes=64)
+        dic_scales = keep.tile([P, DICT_PASSES, Z_DIM], U8, align_bytes=64)
+        xz_codes = keep.tile([P, XZ_PASSES, TOKENS], U32, align_bytes=64)
+        xz_scales = keep.tile([P, XZ_PASSES, TOKENS], U8, align_bytes=64)
+        z_sb = keep.tile([P, ROW_TILES, Z_DIM], F32)
+
+        def empty_bank(bank_in_run, out, in_):
+            if bank_in_run % 4 == 0:
+                nc.vector.tensor_copy(out=out, in_=in_)
+            else:
+                nc.scalar.copy(out=out, in_=in_)
+
+        def transpose_run(raw, passes):
+            grouped_tiles = []
+            for s in range(passes):
+                grouped = grouped_pool.tile([P, PACK * ROWS], BF16, tag="grouped", align_bytes=64)
+                pairs = grouped[:].bitcast(F32).rearrange("p (r u) -> p r u", u=2)
+                for half in range(2):
+                    bank = transposed.tile([P, 2, 2 * P], F32, tag="bank")
+                    for u in range(2):
+                        for i in range(2):
+                            words = raw[:, 2 * half + i, :].bitcast(F32)
+                            first = 2 * s * P
+                            nc.tensor.transpose(
+                                bank[:, u, i * P : (i + 1) * P], words[:, first + u : first + 2 * P : 2], identity[:]
+                            )
+                    empty_bank(
+                        2 * s + half,
+                        pairs[:, half * 2 * P : (half + 1) * 2 * P, :],
+                        bank[:].rearrange("p u r -> p r u"),
+                    )
+                grouped_tiles.append(grouped)
+            return grouped_tiles
+
+        def quantise_run(grouped_tiles, codes, scales, first_pass):
+            for s, grouped in enumerate(grouped_tiles):
+                nc.vector.quantize_mx(
+                    out=codes[:, first_pass + s, :].bitcast(FP8X4),
+                    scales=scales[:, first_pass + s, :],
+                    in_=grouped[:],
+                )
+
+        quantise_run(transpose_run(att_raw[0], RUN_PASSES), att_codes, att_scales, 0)
+        quantise_run(transpose_run(att_raw[1], 1), att_codes, att_scales, RUN_PASSES)
+
+        def regroup_dic(piece):
+            c, h = divmod(piece, 2)
+            grouped = grouped_pool.tile([P, PACK * ROWS], BF16, tag="grouped", align_bytes=64)
+            dst = grouped[:].rearrange("p (c i t) -> p c t i", i=4, t=PACK)
+            src = dic_raw[c][:, :, h * ROWS : (h + 1) * ROWS].rearrange("p t (c i) -> p c t i", i=4)
+            middle = ROWS // 4 // 2
+            nc.vector.tensor_copy(out=dst[:, 0:middle], in_=src[:, 0:middle])
+            nc.scalar.copy(out=dst[:, middle:], in_=src[:, middle:])
+            return grouped
+
+        z_sums = {}
+        for h in range(2):
+            for t in range(ROW_TILES):
+                if h == 0:
+                    bank = transposed.tile([P, ROWS], F32, tag="bank")
+                else:
+                    bank = sums.tile([P, ROWS], F32, tag="sum")
+                z_sums[(t, h)] = bank
+
+        pieces = 2 * DICT_PASSES
+        dic_grouped = [regroup_dic(0)]
+        for piece in range(pieces):
+            c, h = divmod(piece, 2)
+            if piece + 1 < pieces:
+                dic_grouped.append(regroup_dic(piece + 1))
+            columns = slice(h * ROWS, (h + 1) * ROWS)
+            nc.vector.quantize_mx(
+                out=dic_codes[:, c, columns].bitcast(FP8X4),
+                scales=dic_scales[:, c, columns],
+                in_=dic_grouped[piece][:],
+            )
+            for t in range(ROW_TILES):
+                nc.tensor.matmul_mx(
+                    out=z_sums[(t, h)][:],
+                    lhsT=att_codes[:, c, t * P : (t + 1) * P].bitcast(FP8X4),
+                    lhsT_scale=att_scales[:, c, t * P : (t + 1) * P],
+                    rhs=dic_codes[:, c, columns].bitcast(FP8X4),
+                    rhs_scale=dic_scales[:, c, columns],
+                    start=(c == 0),
+                    stop=(c == DICT_PASSES - 1),
+                )
+
+        w_raw.extend([load_w(j) for j in range(FIRST_W_LOADS, W_RUNS)])
+
+        for h in range(2):
+            for t in range(ROW_TILES):
+                empty_bank(t, z_sb[:, t, h * ROWS : (h + 1) * ROWS], z_sums[(t, h)][:])
+        for t in range(ROW_TILES):
+            nc.sync.dma_start(out=z_out[t * P : (t + 1) * P, :], in_=z_sb[:, t, :])
+
+        def transpose_z(s):
+            grouped = grouped_pool.tile([P, PACK * TOKENS], BF16, tag="grouped", align_bytes=64)
+            by_token = grouped[:].rearrange("p (n t) -> p n t", t=PACK)
+            for t in range(ROW_TILES):
+                every_fourth = z_sb[:, t, :].rearrange("p (s q j) -> p s j q", s=Z_PASSES, j=PACK)
+                bank = transposed.tile([P, PACK, P], F32, tag="bank")
+                for j in range(PACK):
+                    nc.tensor.transpose(bank[:, j, :], every_fourth[:, s, j, :], identity[:])
+                empty_bank(t, by_token[:, t * P : (t + 1) * P, :], bank[:].rearrange("p t n -> p n t"))
+            return [grouped]
+
+        w_codes, w_scales, logit_sums = [], [], []
+
+        def prepare_w(j):
+            chunk, r = divmod(j, RUNS_PER_CHUNK)
+            grouped_tiles = transpose_run(w_raw[j], RUN_PASSES)
+            if r == 0:
+                codes = chunk_pool.tile([P, XZ_PASSES, ROWS], U32, tag="w_codes", align_bytes=64)
+                scales = chunk_pool.tile([P, XZ_PASSES, ROWS], U8, tag="w_scales", align_bytes=64)
+                w_codes.append(codes)
+                w_scales.append(scales)
+            quantise_run(grouped_tiles, w_codes[chunk], w_scales[chunk], r * RUN_PASSES)
+
+        def multiply_w(j):
+            chunk, r = divmod(j, RUNS_PER_CHUNK)
+            columns = slice(chunk * ROWS, (chunk + 1) * ROWS)
+            for t in range(ROW_TILES):
+                if r == 0:
+                    bank = sums.tile([P, ROWS], F32, tag="sum")
+                    logit_sums.append(bank)
+                bank = logit_sums[chunk * ROW_TILES + t]
+                for g in range(r * RUN_PASSES, (r + 1) * RUN_PASSES):
+                    nc.tensor.matmul_mx(
+                        out=bank[:],
+                        lhsT=xz_codes[:, g, t * P : (t + 1) * P].bitcast(FP8X4),
+                        lhsT_scale=xz_scales[:, g, t * P : (t + 1) * P],
+                        rhs=w_codes[chunk][:, g, :].bitcast(FP8X4),
+                        rhs_scale=w_scales[chunk][:, g, :],
+                        start=(g == 0),
+                        stop=(g == XZ_PASSES - 1),
+                    )
+                if r == RUNS_PER_CHUNK - 1:
+                    result = result_pool.tile([P, ROWS], F32, tag="result")
+                    nc.vector.tensor_tensor(
+                        out=result[:], in0=bank[:], in1=bias[:, columns], op=mybir.AluOpType.add
+                    )
+                    nc.sync.dma_start(out=logits_out[t * P : (t + 1) * P, columns], in_=result[:])
+
+        for r in range(X_RUNS):
+            quantise_run(transpose_run(x_raw[r], RUN_PASSES), xz_codes, xz_scales, r * RUN_PASSES)
+            prepare_w(r)
+        for j in range(W_RUNS):
+            multiply_w(j)
+            if j < Z_PASSES:
+                quantise_run(transpose_z(j), xz_codes, xz_scales, X_PASSES + j)
+            if j + AHEAD < W_RUNS:
+                prepare_w(j + AHEAD)

@@ -30,7 +30,10 @@ W_RUNS = CHUNKS * RUNS_PER_CHUNK
 X_RUNS = X_PASSES // RUN_PASSES
 AHEAD = 2
 
-FIRST_LOADS = 13
+FIRST_LOADS = 10
+FIRST_SPLIT_RUN = 2
+SPLIT_AHEAD = 2
+
 FIRST_W_LOADS = FIRST_LOADS - 7
 
 FLOPS = 2 * TOKENS * DICT * Z_DIM + 2 * TOKENS * XZ_DIM * OUT_DIM
@@ -44,6 +47,7 @@ def tile_visualdeconfounder_pb_kernel(tc, att_prior, dic, x, cs_w, cs_b, out_0, 
         const = ctx.enter_context(tc.tile_pool(name="const", bufs=1))
         keep = ctx.enter_context(tc.tile_pool(name="keep", bufs=1))
         raw_pool = ctx.enter_context(tc.tile_pool(name="raw", bufs=FIRST_LOADS))
+        split_pool = ctx.enter_context(tc.tile_pool(name="split", bufs=SPLIT_AHEAD + 1))
         grouped_pool = ctx.enter_context(tc.tile_pool(name="grouped", bufs=6))
         chunk_pool = ctx.enter_context(tc.tile_pool(name="chunk", bufs=2))
         result_pool = ctx.enter_context(tc.tile_pool(name="result", bufs=4))
@@ -89,13 +93,21 @@ def tile_visualdeconfounder_pb_kernel(tc, att_prior, dic, x, cs_w, cs_b, out_0, 
         xz_scales = keep.tile([P, XZ_PASSES, TOKENS], U8, align_bytes=64)
         z_sb = keep.tile([P, ROW_TILES, Z_DIM], F32)
 
+        def split_words(raw):
+            split = split_pool.tile([P, ROW_TILES, LOAD_K // 2], F32, tag="split")
+            nc.vector.tensor_copy(
+                out=split[:].rearrange("p t (s u m) -> p (t s) u m", u=2, m=P),
+                in_=raw[:].rearrange("p t k -> p (t k)").bitcast(F32).rearrange("p (a m u) -> p a u m", u=2, m=P),
+            )
+            return split
+
         def empty_bank(bank_in_run, out, in_):
             if bank_in_run % 4 == 0:
                 nc.vector.tensor_copy(out=out, in_=in_)
             else:
                 nc.scalar.copy(out=out, in_=in_)
 
-        def transpose_run(raw, passes):
+        def transpose_run(raw, passes, split=None):
             grouped_tiles = []
             for s in range(passes):
                 grouped = grouped_pool.tile([P, PACK * ROWS], BF16, tag="grouped", align_bytes=64)
@@ -104,13 +116,14 @@ def tile_visualdeconfounder_pb_kernel(tc, att_prior, dic, x, cs_w, cs_b, out_0, 
                     bank = transposed.tile([P, 2, 2 * P], F32, tag="bank")
                     for u in range(2):
                         for i in range(2):
-                            words = raw[:, 2 * half + i, :].bitcast(F32)
                             first = 2 * s * P
-                            nc.tensor.transpose(
-                                bank[:, u, i * P : (i + 1) * P], words[:, first + u : first + 2 * P : 2], identity[:]
-                            )
+                            if split is None:
+                                words = raw[:, 2 * half + i, :].bitcast(F32)[:, first + u : first + 2 * P : 2]
+                            else:
+                                words = split[:, 2 * half + i, first + u * P : first + (u + 1) * P]
+                            nc.tensor.transpose(bank[:, u, i * P : (i + 1) * P], words, identity[:])
                     empty_bank(
-                        2 * s + half,
+                        2 * s + half if split is None else 1,
                         pairs[:, half * 2 * P : (half + 1) * 2 * P, :],
                         bank[:].rearrange("p u r -> p r u"),
                     )
@@ -170,7 +183,7 @@ def tile_visualdeconfounder_pb_kernel(tc, att_prior, dic, x, cs_w, cs_b, out_0, 
                     stop=(c == DICT_PASSES - 1),
                 )
 
-        w_raw.extend([load_w(j) for j in range(FIRST_W_LOADS, W_RUNS)])
+        w_raw.extend([load_w(j) for j in range(FIRST_W_LOADS, FIRST_W_LOADS + 2 + DICT_PASSES)])
 
         for h in range(2):
             for t in range(ROW_TILES):
@@ -190,10 +203,15 @@ def tile_visualdeconfounder_pb_kernel(tc, att_prior, dic, x, cs_w, cs_b, out_0, 
             return [grouped]
 
         w_codes, w_scales, logit_sums = [], [], []
+        w_split = {}
+
+        def split_w(j):
+            if FIRST_SPLIT_RUN <= j < W_RUNS:
+                w_split[j] = split_words(w_raw[j])
 
         def prepare_w(j):
             chunk, r = divmod(j, RUNS_PER_CHUNK)
-            grouped_tiles = transpose_run(w_raw[j], RUN_PASSES)
+            grouped_tiles = transpose_run(w_raw[j], RUN_PASSES, w_split.get(j))
             if r == 0:
                 codes = chunk_pool.tile([P, XZ_PASSES, ROWS], U32, tag="w_codes", align_bytes=64)
                 scales = chunk_pool.tile([P, XZ_PASSES, ROWS], U8, tag="w_scales", align_bytes=64)
@@ -229,9 +247,13 @@ def tile_visualdeconfounder_pb_kernel(tc, att_prior, dic, x, cs_w, cs_b, out_0, 
         for r in range(X_RUNS):
             quantise_run(transpose_run(x_raw[r], RUN_PASSES), xz_codes, xz_scales, r * RUN_PASSES)
             prepare_w(r)
+        w_raw.extend([load_w(j) for j in range(len(w_raw), W_RUNS)])
+        split_w(AHEAD)
+        split_w(AHEAD + 1)
         for j in range(W_RUNS):
             multiply_w(j)
             if j < Z_PASSES:
                 quantise_run(transpose_z(j), xz_codes, xz_scales, X_PASSES + j)
+            split_w(j + AHEAD + SPLIT_AHEAD)
             if j + AHEAD < W_RUNS:
                 prepare_w(j + AHEAD)

@@ -12,6 +12,7 @@ FP8X4 = mybir.dt.float8_e4m3fn_x4
 P = 128
 PACK = 4
 K_PASS = P * PACK
+WORDS = K_PASS // 2
 ROWS = 512
 ROW_TILES = ROWS // P
 
@@ -23,18 +24,14 @@ Z_PASSES = Z_DIM // K_PASS
 XZ_PASSES = XZ_DIM // K_PASS
 
 RUN_PASSES = 2
-LOAD_K = RUN_PASSES * K_PASS
+RUN_K = RUN_PASSES * K_PASS
 RUNS_PER_CHUNK = XZ_PASSES // RUN_PASSES
 CHUNKS = OUT_DIM // ROWS
 W_RUNS = CHUNKS * RUNS_PER_CHUNK
-X_RUNS = X_PASSES // RUN_PASSES
-AHEAD = 2
+PIECES = 2 * DICT_PASSES
 
-FIRST_LOADS = 10
 FIRST_SPLIT_RUN = 2
-SPLIT_AHEAD = 2
-
-FIRST_W_LOADS = FIRST_LOADS - 7
+RAW_BUFFERS = 8
 
 FLOPS = 2 * TOKENS * DICT * Z_DIM + 2 * TOKENS * XZ_DIM * OUT_DIM
 
@@ -46,8 +43,10 @@ def tile_visualdeconfounder_pb_kernel(tc, att_prior, dic, x, cs_w, cs_b, out_0, 
     with ExitStack() as ctx:
         const = ctx.enter_context(tc.tile_pool(name="const", bufs=1))
         keep = ctx.enter_context(tc.tile_pool(name="keep", bufs=1))
-        raw_pool = ctx.enter_context(tc.tile_pool(name="raw", bufs=FIRST_LOADS))
-        split_pool = ctx.enter_context(tc.tile_pool(name="split", bufs=SPLIT_AHEAD + 1))
+        att_pool = ctx.enter_context(tc.tile_pool(name="att", bufs=2))
+        raw_pool = ctx.enter_context(tc.tile_pool(name="raw", bufs=RAW_BUFFERS))
+        split_pool = ctx.enter_context(tc.tile_pool(name="split", bufs=2))
+        z_words_pool = ctx.enter_context(tc.tile_pool(name="z_words", bufs=Z_PASSES))
         grouped_pool = ctx.enter_context(tc.tile_pool(name="grouped", bufs=6))
         chunk_pool = ctx.enter_context(tc.tile_pool(name="chunk", bufs=2))
         result_pool = ctx.enter_context(tc.tile_pool(name="result", bufs=4))
@@ -55,32 +54,45 @@ def tile_visualdeconfounder_pb_kernel(tc, att_prior, dic, x, cs_w, cs_b, out_0, 
         sums = ctx.enter_context(tc.psum_pool(name="sums", bufs=4))
         ctx.enter_context(tc.manual_schedule())
 
-        def load_k_last(matrix, row0, k0, width):
-            raw = raw_pool.tile([P, ROW_TILES, LOAD_K], BF16, tag="raw")
+        def load_att(pair):
+            raw = att_pool.tile([P, 2, DICT], BF16, tag="att_raw")
             nc.sync.dma_start(
-                out=raw[:, :, 0:width],
-                in_=matrix[row0 : row0 + ROWS, k0 : k0 + width].rearrange("(t p) k -> p t k", p=P),
+                out=raw[:], in_=att_prior[pair * 2 * P : (pair + 1) * 2 * P, :].rearrange("(t p) k -> p t k", p=P)
             )
+            return raw
+
+        def load_run(matrix, row0, k0, parts):
+            raw = raw_pool.tile([P, ROW_TILES, RUN_K], BF16, tag="raw")
+            tiles = ROW_TILES // parts
+            for part in range(parts):
+                first = row0 + part * tiles * P
+                nc.sync.dma_start(
+                    out=raw[:, part * tiles : (part + 1) * tiles, :],
+                    in_=matrix[first : first + tiles * P, k0 : k0 + RUN_K].rearrange("(t p) k -> p t k", p=P),
+                )
             return raw
 
         def load_dic(c):
             raw = raw_pool.tile([P, PACK, Z_DIM], BF16, tag="raw")
             nc.sync.dma_start(
-                out=raw[:],
-                in_=dic[c * K_PASS : (c + 1) * K_PASS, :].rearrange("(p t) d -> p t d", t=PACK),
+                out=raw[:], in_=dic[c * K_PASS : (c + 1) * K_PASS, :].rearrange("(p t) d -> p t d", t=PACK)
             )
             return raw
 
         def load_w(j):
             chunk, r = divmod(j, RUNS_PER_CHUNK)
-            return load_k_last(cs_w, chunk * ROWS, r * LOAD_K, LOAD_K)
+            return load_run(cs_w, chunk * ROWS, r * RUN_K, 1)
 
-        att_raw = [load_k_last(att_prior, 0, 0, LOAD_K), load_k_last(att_prior, 0, LOAD_K, DICT - LOAD_K)]
-        dic_raw = [load_dic(c) for c in range(DICT_PASSES)]
-        x_raw = [load_k_last(x, 0, r * LOAD_K, LOAD_K) for r in range(X_DIM // LOAD_K)]
-        w_raw = [load_w(j) for j in range(FIRST_W_LOADS)]
+        dic_raw = [load_dic(0)]
+        att_raw = [load_att(pair) for pair in range(2)]
+        x_raw = [load_run(x, 0, 0, 2)]
+        dic_raw.extend([load_dic(c) for c in range(1, DICT_PASSES)])
+        w_raw = [load_w(0)]
+        x_raw.append(load_run(x, 0, RUN_K, 2))
+        w_raw.append(load_w(1))
         bias = const.tile([P, OUT_DIM], BF16)
         nc.sync.dma_start(out=bias[:], in_=cs_b.partition_broadcast(P))
+        w_raw.append(load_w(2))
 
         identity = const.tile([P, P], F32)
         make_identity(nc, identity[:])
@@ -93,44 +105,50 @@ def tile_visualdeconfounder_pb_kernel(tc, att_prior, dic, x, cs_w, cs_b, out_0, 
         xz_scales = keep.tile([P, XZ_PASSES, TOKENS], U8, align_bytes=64)
         z_sb = keep.tile([P, ROW_TILES, Z_DIM], F32)
 
-        def split_words(raw):
-            split = split_pool.tile([P, ROW_TILES, LOAD_K // 2], F32, tag="split")
-            nc.vector.tensor_copy(
-                out=split[:].rearrange("p t (s u m) -> p (t s) u m", u=2, m=P),
-                in_=raw[:].rearrange("p t k -> p (t k)").bitcast(F32).rearrange("p (a m u) -> p a u m", u=2, m=P),
-            )
-            return split
-
-        def empty_bank(bank_in_run, out, in_):
-            if bank_in_run % 4 == 0:
+        def empty_bank(on_vector, out, in_):
+            if on_vector:
                 nc.vector.tensor_copy(out=out, in_=in_)
             else:
                 nc.scalar.copy(out=out, in_=in_)
 
-        def transpose_run(raw, passes, split=None):
+        def new_grouped():
+            grouped = grouped_pool.tile([P, PACK * ROWS], BF16, tag="grouped", align_bytes=64)
+            return grouped
+
+        def transpose_256_rows(words_of, grouped, half, on_vector):
+            bank = transposed.tile([P, 2, 2 * P], F32, tag="bank")
+            for u in range(2):
+                for i in range(2):
+                    nc.tensor.transpose(bank[:, u, i * P : (i + 1) * P], words_of(2 * half + i, u), identity[:])
+            pairs = grouped[:].bitcast(F32).rearrange("p (r u) -> p r u", u=2)
+            empty_bank(on_vector, pairs[:, half * 2 * P : (half + 1) * 2 * P, :], bank[:].rearrange("p u r -> p r u"))
+
+        def every_second_word(raw, first_tile=0):
+            words = raw[:].rearrange("p t k -> p (t k)").bitcast(F32).rearrange("p (t w) -> p t w", t=raw.shape[1])
+
+            def of_pass(s):
+                return lambda i, u: words[:, i - first_tile, s * WORDS + u : (s + 1) * WORDS : 2]
+
+            return of_pass
+
+        def split_words(raw):
+            split = split_pool.tile([P, ROW_TILES, RUN_PASSES, 2, P], F32, tag="split")
+            nc.vector.tensor_copy(
+                out=split[:].rearrange("p t s u m -> p (t s) u m"),
+                in_=raw[:].rearrange("p t k -> p (t k)").bitcast(F32).rearrange("p (a m u) -> p a u m", u=2, m=P),
+            )
+            return lambda s: lambda i, u: split[:, i, s, u, :]
+
+        def transpose_run(source):
             grouped_tiles = []
-            for s in range(passes):
-                grouped = grouped_pool.tile([P, PACK * ROWS], BF16, tag="grouped", align_bytes=64)
-                pairs = grouped[:].bitcast(F32).rearrange("p (r u) -> p r u", u=2)
+            for s in range(RUN_PASSES):
+                grouped = new_grouped()
                 for half in range(2):
-                    bank = transposed.tile([P, 2, 2 * P], F32, tag="bank")
-                    for u in range(2):
-                        for i in range(2):
-                            first = 2 * s * P
-                            if split is None:
-                                words = raw[:, 2 * half + i, :].bitcast(F32)[:, first + u : first + 2 * P : 2]
-                            else:
-                                words = split[:, 2 * half + i, first + u * P : first + (u + 1) * P]
-                            nc.tensor.transpose(bank[:, u, i * P : (i + 1) * P], words, identity[:])
-                    empty_bank(
-                        2 * s + half if split is None else 1,
-                        pairs[:, half * 2 * P : (half + 1) * 2 * P, :],
-                        bank[:].rearrange("p u r -> p r u"),
-                    )
+                    transpose_256_rows(source(s), grouped, half, False)
                 grouped_tiles.append(grouped)
             return grouped_tiles
 
-        def quantise_run(grouped_tiles, codes, scales, first_pass):
+        def quantise(grouped_tiles, codes, scales, first_pass):
             for s, grouped in enumerate(grouped_tiles):
                 nc.vector.quantize_mx(
                     out=codes[:, first_pass + s, :].bitcast(FP8X4),
@@ -138,12 +156,9 @@ def tile_visualdeconfounder_pb_kernel(tc, att_prior, dic, x, cs_w, cs_b, out_0, 
                     in_=grouped[:],
                 )
 
-        quantise_run(transpose_run(att_raw[0], RUN_PASSES), att_codes, att_scales, 0)
-        quantise_run(transpose_run(att_raw[1], 1), att_codes, att_scales, RUN_PASSES)
-
         def regroup_dic(piece):
             c, h = divmod(piece, 2)
-            grouped = grouped_pool.tile([P, PACK * ROWS], BF16, tag="grouped", align_bytes=64)
+            grouped = new_grouped()
             dst = grouped[:].rearrange("p (c i t) -> p c t i", i=4, t=PACK)
             src = dic_raw[c][:, :, h * ROWS : (h + 1) * ROWS].rearrange("p t (c i) -> p c t i", i=4)
             middle = ROWS // 4 // 2
@@ -151,28 +166,27 @@ def tile_visualdeconfounder_pb_kernel(tc, att_prior, dic, x, cs_w, cs_b, out_0, 
             nc.scalar.copy(out=dst[:, middle:], in_=src[:, middle:])
             return grouped
 
-        z_sums = {}
-        for h in range(2):
-            for t in range(ROW_TILES):
-                if h == 0:
-                    bank = transposed.tile([P, ROWS], F32, tag="bank")
-                else:
-                    bank = sums.tile([P, ROWS], F32, tag="sum")
-                z_sums[(t, h)] = bank
-
-        pieces = 2 * DICT_PASSES
-        dic_grouped = [regroup_dic(0)]
-        for piece in range(pieces):
+        def quantise_dic(piece):
             c, h = divmod(piece, 2)
-            if piece + 1 < pieces:
-                dic_grouped.append(regroup_dic(piece + 1))
             columns = slice(h * ROWS, (h + 1) * ROWS)
             nc.vector.quantize_mx(
                 out=dic_codes[:, c, columns].bitcast(FP8X4),
                 scales=dic_scales[:, c, columns],
                 in_=dic_grouped[piece][:],
             )
+
+        z_sums = {}
+
+        def multiply_dic(piece):
+            c, h = divmod(piece, 2)
+            columns = slice(h * ROWS, (h + 1) * ROWS)
             for t in range(ROW_TILES):
+                if c == 0:
+                    if h == 0:
+                        bank = transposed.tile([P, ROWS], F32, tag="bank")
+                    else:
+                        bank = sums.tile([P, ROWS], F32, tag="sum")
+                    z_sums[(t, h)] = bank
                 nc.tensor.matmul_mx(
                     out=z_sums[(t, h)][:],
                     lhsT=att_codes[:, c, t * P : (t + 1) * P].bitcast(FP8X4),
@@ -183,41 +197,69 @@ def tile_visualdeconfounder_pb_kernel(tc, att_prior, dic, x, cs_w, cs_b, out_0, 
                     stop=(c == DICT_PASSES - 1),
                 )
 
-        w_raw.extend([load_w(j) for j in range(FIRST_W_LOADS, FIRST_W_LOADS + 2 + DICT_PASSES)])
+        dic_grouped = [regroup_dic(piece) for piece in range(2)]
+        for piece in range(2):
+            quantise_dic(piece)
+
+        att_grouped = [new_grouped() for c in range(DICT_PASSES)]
+        for pair in range(2):
+            source = every_second_word(att_raw[pair], 2 * pair)
+            for c in range(DICT_PASSES):
+                transpose_256_rows(source(c), att_grouped[c], pair, c == 0)
+        quantise(att_grouped, att_codes, att_scales, 0)
+
+        quantise(transpose_run(every_second_word(x_raw[0])), xz_codes, xz_scales, 0)
+
+        for piece in range(PIECES):
+            if piece >= 2:
+                quantise_dic(piece)
+            multiply_dic(piece)
+            if piece + 2 < PIECES:
+                dic_grouped.append(regroup_dic(piece + 2))
+
+        w_raw.extend([load_w(j) for j in range(3, 3 + DICT_PASSES + 1)])
 
         for h in range(2):
             for t in range(ROW_TILES):
-                empty_bank(t, z_sb[:, t, h * ROWS : (h + 1) * ROWS], z_sums[(t, h)][:])
-        for t in range(ROW_TILES):
-            nc.sync.dma_start(out=z_out[t * P : (t + 1) * P, :], in_=z_sb[:, t, :])
+                empty_bank(t % 2 == 0, z_sb[:, t, h * ROWS : (h + 1) * ROWS], z_sums[(t, h)][:])
 
-        def transpose_z(s):
-            grouped = grouped_pool.tile([P, PACK * TOKENS], BF16, tag="grouped", align_bytes=64)
-            by_token = grouped[:].rearrange("p (n t) -> p n t", t=PACK)
+        def round_z(s):
+            z_words = z_words_pool.tile([P, ROW_TILES, 2, P, 2], BF16, tag="z_words")
             for t in range(ROW_TILES):
-                every_fourth = z_sb[:, t, :].rearrange("p (s q j) -> p s j q", s=Z_PASSES, j=PACK)
-                bank = transposed.tile([P, PACK, P], F32, tag="bank")
-                for j in range(PACK):
-                    nc.tensor.transpose(bank[:, j, :], every_fourth[:, s, j, :], identity[:])
-                empty_bank(t, by_token[:, t * P : (t + 1) * P, :], bank[:].rearrange("p t n -> p n t"))
+                nc.vector.tensor_copy(
+                    out=z_words[:, t, :, :, :],
+                    in_=z_sb[:, t, s * K_PASS : (s + 1) * K_PASS].rearrange("p (m u e) -> p u m e", u=2, e=2),
+                )
+            return z_words
+
+        def transpose_z(z_words):
+            words = z_words[:].rearrange("p t u m e -> p (t u m e)").bitcast(F32)
+            words = words.rearrange("p (t u m) -> p t u m", t=ROW_TILES, u=2)
+            grouped = new_grouped()
+            for half in range(2):
+                transpose_256_rows(lambda i, u: words[:, i, u, :], grouped, half, False)
             return [grouped]
 
         w_codes, w_scales, logit_sums = [], [], []
-        w_split = {}
+        w_source = {}
 
         def split_w(j):
             if FIRST_SPLIT_RUN <= j < W_RUNS:
-                w_split[j] = split_words(w_raw[j])
+                w_source[j] = split_words(w_raw[j])
 
-        def prepare_w(j):
+        def transpose_w(j):
+            if j < FIRST_SPLIT_RUN:
+                return transpose_run(every_second_word(w_raw[j]))
+            return transpose_run(w_source[j])
+
+        def quantise_w(j, grouped_tiles):
             chunk, r = divmod(j, RUNS_PER_CHUNK)
-            grouped_tiles = transpose_run(w_raw[j], RUN_PASSES, w_split.get(j))
             if r == 0:
                 codes = chunk_pool.tile([P, XZ_PASSES, ROWS], U32, tag="w_codes", align_bytes=64)
                 scales = chunk_pool.tile([P, XZ_PASSES, ROWS], U8, tag="w_scales", align_bytes=64)
                 w_codes.append(codes)
                 w_scales.append(scales)
-            quantise_run(grouped_tiles, w_codes[chunk], w_scales[chunk], r * RUN_PASSES)
+            quantise(grouped_tiles, w_codes[chunk], w_scales[chunk], r * RUN_PASSES)
 
         def multiply_w(j):
             chunk, r = divmod(j, RUNS_PER_CHUNK)
@@ -244,16 +286,28 @@ def tile_visualdeconfounder_pb_kernel(tc, att_prior, dic, x, cs_w, cs_b, out_0, 
                     )
                     nc.sync.dma_start(out=logits_out[t * P : (t + 1) * P, columns], in_=result[:])
 
-        for r in range(X_RUNS):
-            quantise_run(transpose_run(x_raw[r], RUN_PASSES), xz_codes, xz_scales, r * RUN_PASSES)
-            prepare_w(r)
+        w_grouped = transpose_w(0)
+        z_words = [round_z(0)]
+        quantise_w(0, w_grouped)
+        x_grouped = transpose_run(every_second_word(x_raw[1]))
+        z_words.append(round_z(1))
+        quantise(x_grouped, xz_codes, xz_scales, RUN_PASSES)
+
         w_raw.extend([load_w(j) for j in range(len(w_raw), W_RUNS)])
-        split_w(AHEAD)
-        split_w(AHEAD + 1)
-        for j in range(W_RUNS):
+
+        for j in range(Z_PASSES):
+            split_w(j + 2)
+            w_grouped = transpose_w(j + 1)
+            z_grouped = transpose_z(z_words[j])
+            quantise_w(j + 1, w_grouped)
             multiply_w(j)
-            if j < Z_PASSES:
-                quantise_run(transpose_z(j), xz_codes, xz_scales, X_PASSES + j)
-            split_w(j + AHEAD + SPLIT_AHEAD)
-            if j + AHEAD < W_RUNS:
-                prepare_w(j + AHEAD)
+            quantise(z_grouped, xz_codes, xz_scales, X_PASSES + j)
+        split_w(4)
+        quantise_w(3, transpose_w(3))
+        for t in range(ROW_TILES):
+            nc.sync.dma_start(out=z_out[t * P : (t + 1) * P, :], in_=z_sb[:, t, :])
+        for j in range(2, W_RUNS):
+            multiply_w(j)
+            split_w(j + 3)
+            if j + 2 < W_RUNS:
+                quantise_w(j + 2, transpose_w(j + 2))

@@ -90,8 +90,6 @@ def tile_visualdeconfounder_pb_kernel(tc, att_prior, dic, x, cs_w, cs_b, out_0, 
         w_raw = [load_w(0)]
         x_raw.append(load_run(x, 0, RUN_K, 2))
         w_raw.append(load_w(1))
-        bias = const.tile([P, OUT_DIM], BF16)
-        nc.sync.dma_start(out=bias[:], in_=cs_b.partition_broadcast(P))
         w_raw.append(load_w(2))
 
         identity = const.tile([P, P], F32)
@@ -217,7 +215,10 @@ def tile_visualdeconfounder_pb_kernel(tc, att_prior, dic, x, cs_w, cs_b, out_0, 
             if piece + 2 < PIECES:
                 dic_grouped.append(regroup_dic(piece + 2))
 
-        w_raw.extend([load_w(j) for j in range(3, 3 + DICT_PASSES + 1)])
+        w_raw.extend([load_w(j) for j in range(3, 5)])
+        bias = const.tile([P, OUT_DIM], BF16)
+        nc.sync.dma_start(out=bias[:], in_=cs_b.partition_broadcast(P))
+        w_raw.extend([load_w(j) for j in range(5, 3 + DICT_PASSES + 1)])
 
         for h in range(2):
             for t in range(ROW_TILES):

@@ -31,7 +31,9 @@ W_RUNS = CHUNKS * RUNS_PER_CHUNK
 PIECES = 2 * DICT_PASSES
 
 FIRST_SPLIT_RUN = 2
-RAW_BUFFERS = 8
+RAW_BUFFERS = 7
+HALVES = 2
+HALF_TILES = ROW_TILES // HALVES
 
 FLOPS = 2 * TOKENS * DICT * Z_DIM + 2 * TOKENS * XZ_DIM * OUT_DIM
 
@@ -48,7 +50,7 @@ def tile_visualdeconfounder_pb_kernel(tc, att_prior, dic, x, cs_w, cs_b, out_0, 
         split_pool = ctx.enter_context(tc.tile_pool(name="split", bufs=2))
         z_words_pool = ctx.enter_context(tc.tile_pool(name="z_words", bufs=Z_PASSES))
         grouped_pool = ctx.enter_context(tc.tile_pool(name="grouped", bufs=6))
-        chunk_pool = ctx.enter_context(tc.tile_pool(name="chunk", bufs=2))
+        moving_pool = ctx.enter_context(tc.tile_pool(name="moving", bufs=2))
         result_pool = ctx.enter_context(tc.tile_pool(name="result", bufs=4))
         transposed = ctx.enter_context(tc.psum_pool(name="transposed", bufs=4))
         sums = ctx.enter_context(tc.psum_pool(name="sums", bufs=4))
@@ -79,26 +81,29 @@ def tile_visualdeconfounder_pb_kernel(tc, att_prior, dic, x, cs_w, cs_b, out_0, 
             )
             return raw
 
-        def load_w(j):
-            chunk, r = divmod(j, RUNS_PER_CHUNK)
-            return load_run(cs_w, chunk * ROWS, r * RUN_K, 1)
+        def load_w(chunk, half):
+            raw = raw_pool.tile([P, HALF_TILES, XZ_DIM], BF16, tag="raw")
+            first = chunk * ROWS + half * HALF_TILES * P
+            nc.sync.dma_start(
+                out=raw[:], in_=cs_w[first : first + HALF_TILES * P, :].rearrange("(t p) k -> p t k", p=P)
+            )
+            return raw
 
         dic_raw = [load_dic(0)]
         att_raw = [load_att(pair) for pair in range(2)]
         x_raw = [load_run(x, 0, 0, 2)]
         dic_raw.extend([load_dic(c) for c in range(1, DICT_PASSES)])
-        w_raw = [load_w(0)]
+        w_raw = {(0, 0): load_w(0, 0)}
         x_raw.append(load_run(x, 0, RUN_K, 2))
-        w_raw.append(load_w(1))
-        w_raw.append(load_w(2))
+        w_raw[(0, 1)] = load_w(0, 1)
 
         identity = const.tile([P, P], F32)
         make_identity(nc, identity[:])
 
         att_codes = keep.tile([P, DICT_PASSES, TOKENS], U32, align_bytes=64)
         att_scales = keep.tile([P, DICT_PASSES, TOKENS], U8, align_bytes=64)
-        dic_codes = keep.tile([P, DICT_PASSES, Z_DIM], U32, align_bytes=64)
-        dic_scales = keep.tile([P, DICT_PASSES, Z_DIM], U8, align_bytes=64)
+        dic_codes = moving_pool.tile([P, DICT_PASSES, Z_DIM], U32, tag="codes", align_bytes=64)
+        dic_scales = moving_pool.tile([P, DICT_PASSES, Z_DIM], U8, tag="scales", align_bytes=64)
         xz_codes = keep.tile([P, XZ_PASSES, TOKENS], U32, align_bytes=64)
         xz_scales = keep.tile([P, XZ_PASSES, TOKENS], U8, align_bytes=64)
         z_sb = keep.tile([P, ROW_TILES, Z_DIM], F32)
@@ -129,12 +134,28 @@ def tile_visualdeconfounder_pb_kernel(tc, att_prior, dic, x, cs_w, cs_b, out_0, 
 
             return of_pass
 
-        def split_words(raw):
+        def w_words(half, j):
+            chunk, r = divmod(j, RUNS_PER_CHUNK)
+            words = w_raw[(chunk, half)][:].rearrange("p t k -> p (t k)").bitcast(F32)
+            words = words.rearrange("p (t w) -> p t w", t=HALF_TILES)
+            return words[:, :, r * RUN_PASSES * WORDS : (r + 1) * RUN_PASSES * WORDS]
+
+        def every_second_word_of_w(j):
+            halves = [w_words(half, j) for half in range(HALVES)]
+
+            def of_pass(s):
+                return lambda i, u: halves[i // HALF_TILES][:, i % HALF_TILES, s * WORDS + u : (s + 1) * WORDS : 2]
+
+            return of_pass
+
+        def split_words(j):
             split = split_pool.tile([P, ROW_TILES, RUN_PASSES, 2, P], F32, tag="split")
-            nc.vector.tensor_copy(
-                out=split[:].rearrange("p t s u m -> p (t s) u m"),
-                in_=raw[:].rearrange("p t k -> p (t k)").bitcast(F32).rearrange("p (a m u) -> p a u m", u=2, m=P),
-            )
+            for half in range(HALVES):
+                for t in range(HALF_TILES):
+                    nc.vector.tensor_copy(
+                        out=split[:, half * HALF_TILES + t, :, :, :],
+                        in_=w_words(half, j)[:, t, :].rearrange("p (s m u) -> p s u m", u=2, m=P),
+                    )
             return lambda s: lambda i, u: split[:, i, s, u, :]
 
         def transpose_run(source):
@@ -215,10 +236,12 @@ def tile_visualdeconfounder_pb_kernel(tc, att_prior, dic, x, cs_w, cs_b, out_0, 
             if piece + 2 < PIECES:
                 dic_grouped.append(regroup_dic(piece + 2))
 
-        w_raw.extend([load_w(j) for j in range(3, 5)])
+        for half in range(HALVES):
+            w_raw[(1, half)] = load_w(1, half)
         bias = const.tile([P, OUT_DIM], BF16)
         nc.sync.dma_start(out=bias[:], in_=cs_b.partition_broadcast(P))
-        w_raw.extend([load_w(j) for j in range(5, 3 + DICT_PASSES + 1)])
+        for half in range(HALVES):
+            w_raw[(2, half)] = load_w(2, half)
 
         for h in range(2):
             for t in range(ROW_TILES):
@@ -246,18 +269,18 @@ def tile_visualdeconfounder_pb_kernel(tc, att_prior, dic, x, cs_w, cs_b, out_0, 
 
         def split_w(j):
             if FIRST_SPLIT_RUN <= j < W_RUNS:
-                w_source[j] = split_words(w_raw[j])
+                w_source[j] = split_words(j)
 
         def transpose_w(j):
             if j < FIRST_SPLIT_RUN:
-                return transpose_run(every_second_word(w_raw[j]))
+                return transpose_run(every_second_word_of_w(j))
             return transpose_run(w_source[j])
 
         def quantise_w(j, grouped_tiles):
             chunk, r = divmod(j, RUNS_PER_CHUNK)
             if r == 0:
-                codes = chunk_pool.tile([P, XZ_PASSES, ROWS], U32, tag="w_codes", align_bytes=64)
-                scales = chunk_pool.tile([P, XZ_PASSES, ROWS], U8, tag="w_scales", align_bytes=64)
+                codes = moving_pool.tile([P, XZ_PASSES, ROWS], U32, tag="codes", align_bytes=64)
+                scales = moving_pool.tile([P, XZ_PASSES, ROWS], U8, tag="scales", align_bytes=64)
                 w_codes.append(codes)
                 w_scales.append(scales)
             quantise(grouped_tiles, w_codes[chunk], w_scales[chunk], r * RUN_PASSES)
@@ -293,8 +316,6 @@ def tile_visualdeconfounder_pb_kernel(tc, att_prior, dic, x, cs_w, cs_b, out_0, 
         x_grouped = transpose_run(every_second_word(x_raw[1]))
         z_words.append(round_z(1))
         quantise(x_grouped, xz_codes, xz_scales, RUN_PASSES)
-
-        w_raw.extend([load_w(j) for j in range(len(w_raw), W_RUNS)])
 
         for j in range(Z_PASSES):
             split_w(j + 2)

@@ -24,13 +24,11 @@ Z_PASSES = Z_DIM // K_PASS
 XZ_PASSES = XZ_DIM // K_PASS
 
 RUN_PASSES = 2
-RUN_K = RUN_PASSES * K_PASS
 RUNS_PER_CHUNK = XZ_PASSES // RUN_PASSES
 CHUNKS = OUT_DIM // ROWS
 W_RUNS = CHUNKS * RUNS_PER_CHUNK
 PIECES = 2 * DICT_PASSES
 
-FIRST_SPLIT_RUN = 2
 RAW_BUFFERS = 7
 HALVES = 2
 HALF_TILES = ROW_TILES // HALVES
@@ -63,15 +61,12 @@ def tile_visualdeconfounder_pb_kernel(tc, att_prior, dic, x, cs_w, cs_b, out_0, 
             )
             return raw
 
-        def load_run(matrix, row0, k0, parts):
-            raw = raw_pool.tile([P, ROW_TILES, RUN_K], BF16, tag="raw")
-            tiles = ROW_TILES // parts
-            for part in range(parts):
-                first = row0 + part * tiles * P
-                nc.sync.dma_start(
-                    out=raw[:, part * tiles : (part + 1) * tiles, :],
-                    in_=matrix[first : first + tiles * P, k0 : k0 + RUN_K].rearrange("(t p) k -> p t k", p=P),
-                )
+        def load_rows(matrix, half_chunk, width):
+            raw = raw_pool.tile([P, HALF_TILES, width], BF16, tag="raw")
+            first = half_chunk * HALF_TILES * P
+            nc.sync.dma_start(
+                out=raw[:], in_=matrix[first : first + HALF_TILES * P, :].rearrange("(t p) k -> p t k", p=P)
+            )
             return raw
 
         def load_dic(c):
@@ -82,20 +77,14 @@ def tile_visualdeconfounder_pb_kernel(tc, att_prior, dic, x, cs_w, cs_b, out_0, 
             return raw
 
         def load_w(chunk, half):
-            raw = raw_pool.tile([P, HALF_TILES, XZ_DIM], BF16, tag="raw")
-            first = chunk * ROWS + half * HALF_TILES * P
-            nc.sync.dma_start(
-                out=raw[:], in_=cs_w[first : first + HALF_TILES * P, :].rearrange("(t p) k -> p t k", p=P)
-            )
-            return raw
+            return load_rows(cs_w, HALVES * chunk + half, XZ_DIM)
 
         dic_raw = [load_dic(0)]
         att_raw = [load_att(pair) for pair in range(2)]
-        x_raw = [load_run(x, 0, 0, 2)]
+        x_raw = [load_rows(x, 0, X_DIM)]
         dic_raw.extend([load_dic(c) for c in range(1, DICT_PASSES)])
-        w_raw = {(0, 0): load_w(0, 0)}
-        x_raw.append(load_run(x, 0, RUN_K, 2))
-        w_raw[(0, 1)] = load_w(0, 1)
+        x_raw.append(load_rows(x, 1, X_DIM))
+        w_raw = {(0, half): load_w(0, half) for half in range(HALVES)}
 
         identity = const.tile([P, P], F32)
         make_identity(nc, identity[:])
@@ -118,54 +107,52 @@ def tile_visualdeconfounder_pb_kernel(tc, att_prior, dic, x, cs_w, cs_b, out_0, 
             grouped = grouped_pool.tile([P, PACK * ROWS], BF16, tag="grouped", align_bytes=64)
             return grouped
 
-        def transpose_256_rows(words_of, grouped, half, on_vector):
+        def transpose_256_rows(words_of, grouped, part, on_vector):
             bank = transposed.tile([P, 2, 2 * P], F32, tag="bank")
             for u in range(2):
                 for i in range(2):
-                    nc.tensor.transpose(bank[:, u, i * P : (i + 1) * P], words_of(2 * half + i, u), identity[:])
+                    nc.tensor.transpose(bank[:, u, i * P : (i + 1) * P], words_of(i, u), identity[:])
             pairs = grouped[:].bitcast(F32).rearrange("p (r u) -> p r u", u=2)
-            empty_bank(on_vector, pairs[:, half * 2 * P : (half + 1) * 2 * P, :], bank[:].rearrange("p u r -> p r u"))
+            empty_bank(on_vector, pairs[:, part * 2 * P : (part + 1) * 2 * P, :], bank[:].rearrange("p u r -> p r u"))
 
-        def every_second_word(raw, first_tile=0):
-            words = raw[:].rearrange("p t k -> p (t k)").bitcast(F32).rearrange("p (t w) -> p t w", t=raw.shape[1])
+        def words_of_rows(raw):
+            words = raw[:].rearrange("p t k -> p (t k)").bitcast(F32)
+            return words.rearrange("p (t w) -> p t w", t=HALF_TILES)
 
-            def of_pass(s):
-                return lambda i, u: words[:, i - first_tile, s * WORDS + u : (s + 1) * WORDS : 2]
-
-            return of_pass
-
-        def w_words(half, j):
-            chunk, r = divmod(j, RUNS_PER_CHUNK)
-            words = w_raw[(chunk, half)][:].rearrange("p t k -> p (t k)").bitcast(F32)
-            words = words.rearrange("p (t w) -> p t w", t=HALF_TILES)
-            return words[:, :, r * RUN_PASSES * WORDS : (r + 1) * RUN_PASSES * WORDS]
-
-        def every_second_word_of_w(j):
-            halves = [w_words(half, j) for half in range(HALVES)]
-
-            def of_pass(s):
-                return lambda i, u: halves[i // HALF_TILES][:, i % HALF_TILES, s * WORDS + u : (s + 1) * WORDS : 2]
-
-            return of_pass
+        def every_second_word(words, g):
+            return lambda i, u: words[:, i, g * WORDS + u : (g + 1) * WORDS : 2]
 
         def split_words(j):
+            chunk, r = divmod(j, RUNS_PER_CHUNK)
             split = split_pool.tile([P, ROW_TILES, RUN_PASSES, 2, P], F32, tag="split")
-            for half in range(HALVES):
-                for t in range(HALF_TILES):
-                    nc.vector.tensor_copy(
-                        out=split[:, half * HALF_TILES + t, :, :, :],
-                        in_=w_words(half, j)[:, t, :].rearrange("p (s m u) -> p s u m", u=2, m=P),
-                    )
-            return lambda s: lambda i, u: split[:, i, s, u, :]
+            for t in range(ROW_TILES):
+                words = words_of_rows(w_raw[(chunk, t // HALF_TILES)])[:, t % HALF_TILES, :]
+                nc.vector.tensor_copy(
+                    out=split[:, t, :, :, :],
+                    in_=words[:, r * RUN_PASSES * WORDS : (r + 1) * RUN_PASSES * WORDS].rearrange(
+                        "p (s m u) -> p s u m", u=2, m=P
+                    ),
+                )
+            return split
 
-        def transpose_run(source):
+        def transpose_half(words):
             grouped_tiles = []
-            for s in range(RUN_PASSES):
-                grouped = new_grouped()
-                for half in range(2):
-                    transpose_256_rows(source(s), grouped, half, False)
-                grouped_tiles.append(grouped)
+            for g in range(X_PASSES):
+                if g % 2 == 0:
+                    grouped = new_grouped()
+                    grouped_tiles.append(grouped)
+                transpose_256_rows(every_second_word(words, g), grouped, g % 2, False)
             return grouped_tiles
+
+        def quantise_half(half, grouped_tiles, codes, scales):
+            columns = slice(half * HALF_TILES * P, (half + 1) * HALF_TILES * P)
+            width = PACK * HALF_TILES * P
+            for g in range(X_PASSES):
+                nc.vector.quantize_mx(
+                    out=codes[:, g, columns].bitcast(FP8X4),
+                    scales=scales[:, g, columns],
+                    in_=grouped_tiles[g // 2][:, (g % 2) * width : (g % 2 + 1) * width],
+                )
 
         def quantise(grouped_tiles, codes, scales, first_pass):
             for s, grouped in enumerate(grouped_tiles):
@@ -222,12 +209,12 @@ def tile_visualdeconfounder_pb_kernel(tc, att_prior, dic, x, cs_w, cs_b, out_0, 
 
         att_grouped = [new_grouped() for c in range(DICT_PASSES)]
         for pair in range(2):
-            source = every_second_word(att_raw[pair], 2 * pair)
+            words = words_of_rows(att_raw[pair])
             for c in range(DICT_PASSES):
-                transpose_256_rows(source(c), att_grouped[c], pair, c == 0)
+                transpose_256_rows(every_second_word(words, c), att_grouped[c], pair, c == 0)
         quantise(att_grouped, att_codes, att_scales, 0)
 
-        quantise(transpose_run(every_second_word(x_raw[0])), xz_codes, xz_scales, 0)
+        quantise_half(0, transpose_half(words_of_rows(x_raw[0])), xz_codes, xz_scales)
 
         for piece in range(PIECES):
             if piece >= 2:
@@ -260,29 +247,38 @@ def tile_visualdeconfounder_pb_kernel(tc, att_prior, dic, x, cs_w, cs_b, out_0, 
             words = z_words[:].rearrange("p t u m e -> p (t u m e)").bitcast(F32)
             words = words.rearrange("p (t u m) -> p t u m", t=ROW_TILES, u=2)
             grouped = new_grouped()
-            for half in range(2):
-                transpose_256_rows(lambda i, u: words[:, i, u, :], grouped, half, False)
+            for half in range(HALVES):
+                own = words[:, half * HALF_TILES : (half + 1) * HALF_TILES]
+                transpose_256_rows(lambda i, u: own[:, i, u, :], grouped, half, False)
             return [grouped]
 
         w_codes, w_scales, logit_sums = [], [], []
         w_source = {}
 
         def split_w(j):
-            if FIRST_SPLIT_RUN <= j < W_RUNS:
+            if j < W_RUNS:
                 w_source[j] = split_words(j)
 
+        def new_chunk():
+            codes = moving_pool.tile([P, XZ_PASSES, ROWS], U32, tag="codes", align_bytes=64)
+            scales = moving_pool.tile([P, XZ_PASSES, ROWS], U8, tag="scales", align_bytes=64)
+            w_codes.append(codes)
+            w_scales.append(scales)
+
         def transpose_w(j):
-            if j < FIRST_SPLIT_RUN:
-                return transpose_run(every_second_word_of_w(j))
-            return transpose_run(w_source[j])
+            grouped_tiles = []
+            for s in range(RUN_PASSES):
+                grouped = new_grouped()
+                for half in range(HALVES):
+                    own = w_source[j][:, half * HALF_TILES : (half + 1) * HALF_TILES, s, :, :]
+                    transpose_256_rows(lambda i, u: own[:, i, u, :], grouped, half, False)
+                grouped_tiles.append(grouped)
+            return grouped_tiles
 
         def quantise_w(j, grouped_tiles):
             chunk, r = divmod(j, RUNS_PER_CHUNK)
             if r == 0:
-                codes = moving_pool.tile([P, XZ_PASSES, ROWS], U32, tag="codes", align_bytes=64)
-                scales = moving_pool.tile([P, XZ_PASSES, ROWS], U8, tag="scales", align_bytes=64)
-                w_codes.append(codes)
-                w_scales.append(scales)
+                new_chunk()
             quantise(grouped_tiles, w_codes[chunk], w_scales[chunk], r * RUN_PASSES)
 
         def multiply_w(j):
@@ -310,20 +306,25 @@ def tile_visualdeconfounder_pb_kernel(tc, att_prior, dic, x, cs_w, cs_b, out_0, 
                     )
                     nc.sync.dma_start(out=logits_out[t * P : (t + 1) * P, columns], in_=result[:])
 
-        w_grouped = transpose_w(0)
+        x_grouped = transpose_half(words_of_rows(x_raw[1]))
         z_words = [round_z(0)]
-        quantise_w(0, w_grouped)
-        x_grouped = transpose_run(every_second_word(x_raw[1]))
+        quantise_half(1, x_grouped, xz_codes, xz_scales)
+        new_chunk()
+        w_grouped = transpose_half(words_of_rows(w_raw[(0, 0)]))
         z_words.append(round_z(1))
-        quantise(x_grouped, xz_codes, xz_scales, RUN_PASSES)
-
-        for j in range(Z_PASSES):
-            split_w(j + 2)
-            w_grouped = transpose_w(j + 1)
-            z_grouped = transpose_z(z_words[j])
-            quantise_w(j + 1, w_grouped)
-            multiply_w(j)
-            quantise(z_grouped, xz_codes, xz_scales, X_PASSES + j)
+        quantise_half(0, w_grouped, w_codes[0], w_scales[0])
+        split_w(2)
+        w_grouped = transpose_half(words_of_rows(w_raw[(0, 1)]))
+        z_grouped = transpose_z(z_words[0])
+        quantise_half(1, w_grouped, w_codes[0], w_scales[0])
+        multiply_w(0)
+        quantise(z_grouped, xz_codes, xz_scales, X_PASSES)
+        split_w(3)
+        w_grouped = transpose_w(2)
+        z_grouped = transpose_z(z_words[1])
+        quantise_w(2, w_grouped)
+        multiply_w(1)
+        quantise(z_grouped, xz_codes, xz_scales, X_PASSES + 1)
         split_w(4)
         quantise_w(3, transpose_w(3))
         for t in range(ROW_TILES):

@@ -24,14 +24,17 @@ Z_PASSES = Z_DIM // K_PASS
 XZ_PASSES = XZ_DIM // K_PASS
 
 RUN_PASSES = 2
+X_RUNS = X_PASSES // RUN_PASSES
 RUNS_PER_CHUNK = XZ_PASSES // RUN_PASSES
 CHUNKS = OUT_DIM // ROWS
 W_RUNS = CHUNKS * RUNS_PER_CHUNK
 PIECES = 2 * DICT_PASSES
 
+FIRST_Z_RUN = X_RUNS
 RAW_BUFFERS = 7
 HALVES = 2
 HALF_TILES = ROW_TILES // HALVES
+HALF_ROWS = HALF_TILES * P
 
 FLOPS = 2 * TOKENS * DICT * Z_DIM + 2 * TOKENS * XZ_DIM * OUT_DIM
 
@@ -61,11 +64,10 @@ def tile_visualdeconfounder_pb_kernel(tc, att_prior, dic, x, cs_w, cs_b, out_0, 
             )
             return raw
 
-        def load_rows(matrix, half_chunk, width):
-            raw = raw_pool.tile([P, HALF_TILES, width], BF16, tag="raw")
-            first = half_chunk * HALF_TILES * P
+        def load_rows(matrix, first, tiles, columns):
+            raw = raw_pool.tile([P, tiles, columns.stop - columns.start], BF16, tag="raw")
             nc.sync.dma_start(
-                out=raw[:], in_=matrix[first : first + HALF_TILES * P, :].rearrange("(t p) k -> p t k", p=P)
+                out=raw[:], in_=matrix[first : first + tiles * P, columns].rearrange("(t p) k -> p t k", p=P)
             )
             return raw
 
@@ -76,15 +78,18 @@ def tile_visualdeconfounder_pb_kernel(tc, att_prior, dic, x, cs_w, cs_b, out_0, 
             )
             return raw
 
-        def load_w(chunk, half):
-            return load_rows(cs_w, HALVES * chunk + half, XZ_DIM)
+        def load_x(half):
+            return load_rows(x, half * HALF_ROWS, HALF_TILES, slice(0, X_DIM))
+
+        def load_w(chunk, half, columns):
+            return load_rows(cs_w, chunk * ROWS + half * HALF_ROWS, HALF_TILES, columns)
 
         dic_raw = [load_dic(0)]
         att_raw = [load_att(pair) for pair in range(2)]
-        x_raw = [load_rows(x, 0, X_DIM)]
+        x_raw = [load_x(0)]
         dic_raw.extend([load_dic(c) for c in range(1, DICT_PASSES)])
-        x_raw.append(load_rows(x, 1, X_DIM))
-        w_raw = {(0, half): load_w(0, half) for half in range(HALVES)}
+        x_raw.append(load_x(1))
+        w_raw = {(0, half): load_w(0, half, slice(0, X_DIM)) for half in range(HALVES)}
 
         identity = const.tile([P, P], F32)
         make_identity(nc, identity[:])
@@ -117,41 +122,46 @@ def tile_visualdeconfounder_pb_kernel(tc, att_prior, dic, x, cs_w, cs_b, out_0, 
 
         def words_of_rows(raw):
             words = raw[:].rearrange("p t k -> p (t k)").bitcast(F32)
-            return words.rearrange("p (t w) -> p t w", t=HALF_TILES)
+            return words.rearrange("p (t w) -> p t w", t=raw.shape[1])
 
-        def every_second_word(words, g):
-            return lambda i, u: words[:, i, g * WORDS + u : (g + 1) * WORDS : 2]
+        def every_second_word(words):
+            return lambda g: lambda i, u: words[:, i, g * WORDS + u : (g + 1) * WORDS : 2]
 
         def split_words(j):
             chunk, r = divmod(j, RUNS_PER_CHUNK)
             split = split_pool.tile([P, ROW_TILES, RUN_PASSES, 2, P], F32, tag="split")
             for t in range(ROW_TILES):
-                words = words_of_rows(w_raw[(chunk, t // HALF_TILES)])[:, t % HALF_TILES, :]
+                if j == FIRST_Z_RUN:
+                    words = words_of_rows(w_raw_z)[:, t, :]
+                else:
+                    words = words_of_rows(w_raw[(chunk, t // HALF_TILES)])[:, t % HALF_TILES, :]
+                    words = words[:, r * RUN_PASSES * WORDS : (r + 1) * RUN_PASSES * WORDS]
                 nc.vector.tensor_copy(
-                    out=split[:, t, :, :, :],
-                    in_=words[:, r * RUN_PASSES * WORDS : (r + 1) * RUN_PASSES * WORDS].rearrange(
-                        "p (s m u) -> p s u m", u=2, m=P
-                    ),
+                    out=split[:, t, :, :, :], in_=words.rearrange("p (s m u) -> p s u m", u=2, m=P)
                 )
             return split
 
-        def transpose_half(words):
-            grouped_tiles = []
-            for g in range(X_PASSES):
-                if g % 2 == 0:
-                    grouped = new_grouped()
-                    grouped_tiles.append(grouped)
-                transpose_256_rows(every_second_word(words, g), grouped, g % 2, False)
-            return grouped_tiles
+        def split_half(words):
+            split = split_pool.tile([P, HALF_TILES, X_PASSES, 2, P], F32, tag="split")
+            src = words[:, :, 0 : X_PASSES * WORDS].rearrange("p t (s m u) -> p t s u m", u=2, m=P)
+            nc.scalar.copy(out=split[:, 0, :, :, :], in_=src[:, 0])
+            nc.vector.tensor_copy(out=split[:, 1, :, :, :], in_=src[:, 1])
+            return lambda g: lambda i, u: split[:, i, g, u, :]
 
-        def quantise_half(half, grouped_tiles, codes, scales):
-            columns = slice(half * HALF_TILES * P, (half + 1) * HALF_TILES * P)
-            width = PACK * HALF_TILES * P
-            for g in range(X_PASSES):
+        def transpose_pair(source_of, r):
+            grouped = new_grouped()
+            for s in range(RUN_PASSES):
+                transpose_256_rows(source_of(r * RUN_PASSES + s), grouped, s, False)
+            return grouped
+
+        def quantise_pair(half, r, grouped, codes, scales):
+            columns = slice(half * HALF_ROWS, (half + 1) * HALF_ROWS)
+            width = PACK * HALF_ROWS
+            for s in range(RUN_PASSES):
                 nc.vector.quantize_mx(
-                    out=codes[:, g, columns].bitcast(FP8X4),
-                    scales=scales[:, g, columns],
-                    in_=grouped_tiles[g // 2][:, (g % 2) * width : (g % 2 + 1) * width],
+                    out=codes[:, r * RUN_PASSES + s, columns].bitcast(FP8X4),
+                    scales=scales[:, r * RUN_PASSES + s, columns],
+                    in_=grouped[:, s * width : (s + 1) * width],
                 )
 
         def quantise(grouped_tiles, codes, scales, first_pass):
@@ -209,12 +219,14 @@ def tile_visualdeconfounder_pb_kernel(tc, att_prior, dic, x, cs_w, cs_b, out_0, 
 
         att_grouped = [new_grouped() for c in range(DICT_PASSES)]
         for pair in range(2):
-            words = words_of_rows(att_raw[pair])
+            source_of = every_second_word(words_of_rows(att_raw[pair]))
             for c in range(DICT_PASSES):
-                transpose_256_rows(every_second_word(words, c), att_grouped[c], pair, c == 0)
+                transpose_256_rows(source_of(c), att_grouped[c], pair, c == 0)
         quantise(att_grouped, att_codes, att_scales, 0)
 
-        quantise_half(0, transpose_half(words_of_rows(x_raw[0])), xz_codes, xz_scales)
+        x_source = every_second_word(words_of_rows(x_raw[0]))
+        for r in range(X_RUNS):
+            quantise_pair(0, r, transpose_pair(x_source, r), xz_codes, xz_scales)
 
         for piece in range(PIECES):
             if piece >= 2:
@@ -223,13 +235,15 @@ def tile_visualdeconfounder_pb_kernel(tc, att_prior, dic, x, cs_w, cs_b, out_0, 
             if piece + 2 < PIECES:
                 dic_grouped.append(regroup_dic(piece + 2))
 
+        w_raw_z = load_rows(cs_w, 0, ROW_TILES, slice(X_DIM, XZ_DIM))
         for half in range(HALVES):
-            w_raw[(1, half)] = load_w(1, half)
+            w_raw[(1, half)] = load_w(1, half, slice(0, XZ_DIM))
         bias = const.tile([P, OUT_DIM], BF16)
         nc.sync.dma_start(out=bias[:], in_=cs_b.partition_broadcast(P))
         for half in range(HALVES):
-            w_raw[(2, half)] = load_w(2, half)
+            w_raw[(2, half)] = load_w(2, half, slice(0, XZ_DIM))
 
+        x_source = split_half(words_of_rows(x_raw[1]))
         for h in range(2):
             for t in range(ROW_TILES):
                 empty_bank(t % 2 == 0, z_sb[:, t, h * ROWS : (h + 1) * ROWS], z_sums[(t, h)][:])
@@ -306,25 +320,32 @@ def tile_visualdeconfounder_pb_kernel(tc, att_prior, dic, x, cs_w, cs_b, out_0, 
                     )
                     nc.sync.dma_start(out=logits_out[t * P : (t + 1) * P, columns], in_=result[:])
 
-        x_grouped = transpose_half(words_of_rows(x_raw[1]))
-        z_words = [round_z(0)]
-        quantise_half(1, x_grouped, xz_codes, xz_scales)
         new_chunk()
-        w_grouped = transpose_half(words_of_rows(w_raw[(0, 0)]))
-        z_words.append(round_z(1))
-        quantise_half(0, w_grouped, w_codes[0], w_scales[0])
+        w_sources = [every_second_word(words_of_rows(w_raw[(0, half)])) for half in range(HALVES)]
+
+        def prepare_x(r):
+            quantise_pair(1, r, transpose_pair(x_source, r), xz_codes, xz_scales)
+
+        def prepare_first(half, r):
+            quantise_pair(half, r, transpose_pair(w_sources[half], r), w_codes[0], w_scales[0])
+
+        prepare_x(0)
+        prepare_first(0, 0)
+        prepare_x(1)
+        prepare_first(1, 0)
+        prepare_first(0, 1)
         split_w(2)
-        w_grouped = transpose_half(words_of_rows(w_raw[(0, 1)]))
-        z_grouped = transpose_z(z_words[0])
-        quantise_half(1, w_grouped, w_codes[0], w_scales[0])
+        z_words = [round_z(0)]
         multiply_w(0)
-        quantise(z_grouped, xz_codes, xz_scales, X_PASSES)
-        split_w(3)
+        prepare_first(1, 1)
+        z_words.append(round_z(1))
         w_grouped = transpose_w(2)
-        z_grouped = transpose_z(z_words[1])
+        z_grouped = transpose_z(z_words[0])
         quantise_w(2, w_grouped)
+        split_w(3)
+        quantise(z_grouped, xz_codes, xz_scales, X_PASSES)
         multiply_w(1)
-        quantise(z_grouped, xz_codes, xz_scales, X_PASSES + 1)
+        quantise(transpose_z(z_words[1]), xz_codes, xz_scales, X_PASSES + 1)
         split_w(4)
         quantise_w(3, transpose_w(3))
         for t in range(ROW_TILES):

@@ -50,7 +50,7 @@ def tile_visualdeconfounder_pb_kernel(tc, att_prior, dic, x, cs_w, cs_b, out_0, 
         raw_pool = ctx.enter_context(tc.tile_pool(name="raw", bufs=RAW_BUFFERS))
         split_pool = ctx.enter_context(tc.tile_pool(name="split", bufs=2))
         z_words_pool = ctx.enter_context(tc.tile_pool(name="z_words", bufs=Z_PASSES))
-        grouped_pool = ctx.enter_context(tc.tile_pool(name="grouped", bufs=6))
+        grouped_pool = ctx.enter_context(tc.tile_pool(name="grouped", bufs=7))
         moving_pool = ctx.enter_context(tc.tile_pool(name="moving", bufs=2))
         result_pool = ctx.enter_context(tc.tile_pool(name="result", bufs=4))
         transposed = ctx.enter_context(tc.psum_pool(name="transposed", bufs=4))
@@ -148,10 +148,10 @@ def tile_visualdeconfounder_pb_kernel(tc, att_prior, dic, x, cs_w, cs_b, out_0, 
             nc.vector.tensor_copy(out=split[:, 1, :, :, :], in_=src[:, 1])
             return lambda g: lambda i, u: split[:, i, g, u, :]
 
-        def transpose_pair(source_of, r):
+        def transpose_pair(source_of, r, last_on_vector=False):
             grouped = new_grouped()
             for s in range(RUN_PASSES):
-                transpose_256_rows(source_of(r * RUN_PASSES + s), grouped, s, False)
+                transpose_256_rows(source_of(r * RUN_PASSES + s), grouped, s, last_on_vector and s == RUN_PASSES - 1)
             return grouped
 
         def quantise_pair(half, r, grouped, codes, scales):
@@ -225,8 +225,7 @@ def tile_visualdeconfounder_pb_kernel(tc, att_prior, dic, x, cs_w, cs_b, out_0, 
         quantise(att_grouped, att_codes, att_scales, 0)
 
         x_source = every_second_word(words_of_rows(x_raw[0]))
-        for r in range(X_RUNS):
-            quantise_pair(0, r, transpose_pair(x_source, r), xz_codes, xz_scales)
+        x_grouped = [transpose_pair(x_source, r) for r in range(X_RUNS)]
 
         for piece in range(PIECES):
             if piece >= 2:
@@ -234,6 +233,8 @@ def tile_visualdeconfounder_pb_kernel(tc, att_prior, dic, x, cs_w, cs_b, out_0, 
             multiply_dic(piece)
             if piece + 2 < PIECES:
                 dic_grouped.append(regroup_dic(piece + 2))
+            if piece < X_RUNS:
+                quantise_pair(0, piece, x_grouped[piece], xz_codes, xz_scales)
 
         w_raw_z = load_rows(cs_w, 0, ROW_TILES, slice(X_DIM, XZ_DIM))
         for half in range(HALVES):
@@ -295,25 +296,33 @@ def tile_visualdeconfounder_pb_kernel(tc, att_prior, dic, x, cs_w, cs_b, out_0, 
                 new_chunk()
             quantise(grouped_tiles, w_codes[chunk], w_scales[chunk], r * RUN_PASSES)
 
+        def multiply_one(chunk, g, t):
+            if g == 0:
+                bank = sums.tile([P, ROWS], F32, tag="sum")
+                logit_sums.append(bank)
+            nc.tensor.matmul_mx(
+                out=logit_sums[chunk * ROW_TILES + t][:],
+                lhsT=xz_codes[:, g, t * P : (t + 1) * P].bitcast(FP8X4),
+                lhsT_scale=xz_scales[:, g, t * P : (t + 1) * P],
+                rhs=w_codes[chunk][:, g, :].bitcast(FP8X4),
+                rhs_scale=w_scales[chunk][:, g, :],
+                start=(g == 0),
+                stop=(g == XZ_PASSES - 1),
+            )
+
+        def multiply_pass_of_w(j, s):
+            chunk, r = divmod(j, RUNS_PER_CHUNK)
+            for t in range(ROW_TILES):
+                multiply_one(chunk, r * RUN_PASSES + s, t)
+
         def multiply_w(j):
             chunk, r = divmod(j, RUNS_PER_CHUNK)
             columns = slice(chunk * ROWS, (chunk + 1) * ROWS)
             for t in range(ROW_TILES):
-                if r == 0:
-                    bank = sums.tile([P, ROWS], F32, tag="sum")
-                    logit_sums.append(bank)
-                bank = logit_sums[chunk * ROW_TILES + t]
                 for g in range(r * RUN_PASSES, (r + 1) * RUN_PASSES):
-                    nc.tensor.matmul_mx(
-                        out=bank[:],
-                        lhsT=xz_codes[:, g, t * P : (t + 1) * P].bitcast(FP8X4),
-                        lhsT_scale=xz_scales[:, g, t * P : (t + 1) * P],
-                        rhs=w_codes[chunk][:, g, :].bitcast(FP8X4),
-                        rhs_scale=w_scales[chunk][:, g, :],
-                        start=(g == 0),
-                        stop=(g == XZ_PASSES - 1),
-                    )
+                    multiply_one(chunk, g, t)
                 if r == RUNS_PER_CHUNK - 1:
+                    bank = logit_sums[chunk * ROW_TILES + t]
                     result = result_pool.tile([P, ROWS], F32, tag="result")
                     nc.vector.tensor_tensor(
                         out=result[:], in0=bank[:], in1=bias[:, columns], op=mybir.AluOpType.add
@@ -324,7 +333,7 @@ def tile_visualdeconfounder_pb_kernel(tc, att_prior, dic, x, cs_w, cs_b, out_0, 
         w_sources = [every_second_word(words_of_rows(w_raw[(0, half)])) for half in range(HALVES)]
 
         def prepare_x(r):
-            quantise_pair(1, r, transpose_pair(x_source, r), xz_codes, xz_scales)
+            quantise_pair(1, r, transpose_pair(x_source, r, True), xz_codes, xz_scales)
 
         def prepare_first(half, r):
             quantise_pair(half, r, transpose_pair(w_sources[half], r), w_codes[0], w_scales[0])
@@ -335,17 +344,16 @@ def tile_visualdeconfounder_pb_kernel(tc, att_prior, dic, x, cs_w, cs_b, out_0, 
         prepare_first(1, 0)
         prepare_first(0, 1)
         split_w(2)
-        z_words = [round_z(0)]
-        multiply_w(0)
         prepare_first(1, 1)
-        z_words.append(round_z(1))
-        w_grouped = transpose_w(2)
-        z_grouped = transpose_z(z_words[0])
-        quantise_w(2, w_grouped)
+        multiply_w(0)
+        z_words = [round_z(s) for s in range(Z_PASSES)]
+        quantise_w(2, transpose_w(2))
         split_w(3)
-        quantise(z_grouped, xz_codes, xz_scales, X_PASSES)
-        multiply_w(1)
-        quantise(transpose_z(z_words[1]), xz_codes, xz_scales, X_PASSES + 1)
+        multiply_pass_of_w(1, 0)
+        z_grouped = [transpose_z(z_words[s]) for s in range(Z_PASSES)]
+        for s in range(Z_PASSES):
+            quantise(z_grouped[s], xz_codes, xz_scales, X_PASSES + s)
+        multiply_pass_of_w(1, 1)
         split_w(4)
         quantise_w(3, transpose_w(3))
         for t in range(ROW_TILES):

from contextlib import ExitStack

import concourse.mybir as mybir
from concourse.masks import make_identity

F32 = mybir.dt.float32
BF16 = mybir.dt.bfloat16
U32 = mybir.dt.uint32
U8 = mybir.dt.uint8
FP8X4 = mybir.dt.float8_e4m3fn_x4

P = 128
PACK = 4
K_PASS = P * PACK
WORDS = K_PASS // 2
ROWS = 512
ROW_TILES = ROWS // P

TOKENS, DICT, Z_DIM, X_DIM, OUT_DIM = 512, 1536, 1024, 2048, 1536
XZ_DIM = X_DIM + Z_DIM
DICT_PASSES = DICT // K_PASS
X_PASSES = X_DIM // K_PASS
Z_PASSES = Z_DIM // K_PASS
XZ_PASSES = XZ_DIM // K_PASS

RUN_PASSES = 2
X_RUNS = X_PASSES // RUN_PASSES
RUNS_PER_CHUNK = XZ_PASSES // RUN_PASSES
CHUNKS = OUT_DIM // ROWS
W_RUNS = CHUNKS * RUNS_PER_CHUNK
PIECES = 2 * DICT_PASSES

FIRST_Z_RUN = X_RUNS
RAW_BUFFERS = 7
HALVES = 2
HALF_TILES = ROW_TILES // HALVES
HALF_ROWS = HALF_TILES * P

FLOPS = 2 * TOKENS * DICT * Z_DIM + 2 * TOKENS * XZ_DIM * OUT_DIM


def tile_visualdeconfounder_pb_kernel(tc, att_prior, dic, x, cs_w, cs_b, out_0, out_1):
    nc = tc.nc
    logits_out, z_out = out_0, out_1

    with ExitStack() as ctx:
        const = ctx.enter_context(tc.tile_pool(name="const", bufs=1))
        keep = ctx.enter_context(tc.tile_pool(name="keep", bufs=1))
        att_pool = ctx.enter_context(tc.tile_pool(name="att", bufs=2))
        raw_pool = ctx.enter_context(tc.tile_pool(name="raw", bufs=RAW_BUFFERS))
        split_pool = ctx.enter_context(tc.tile_pool(name="split", bufs=2))
        z_words_pool = ctx.enter_context(tc.tile_pool(name="z_words", bufs=Z_PASSES))
        grouped_pool = ctx.enter_context(tc.tile_pool(name="grouped", bufs=7))
        moving_pool = ctx.enter_context(tc.tile_pool(name="moving", bufs=2))
        result_pool = ctx.enter_context(tc.tile_pool(name="result", bufs=4))
        transposed = ctx.enter_context(tc.psum_pool(name="transposed", bufs=4))
        sums = ctx.enter_context(tc.psum_pool(name="sums", bufs=4))
        ctx.enter_context(tc.manual_schedule())

        def load_att(pair):
            raw = att_pool.tile([P, 2, DICT], BF16, tag="att_raw")
            nc.sync.dma_start(
                out=raw[:], in_=att_prior[pair * 2 * P : (pair + 1) * 2 * P, :].rearrange("(t p) k -> p t k", p=P)
            )
            return raw

        def load_rows(matrix, first, tiles, columns):
            raw = raw_pool.tile([P, tiles, columns.stop - columns.start], BF16, tag="raw")
            nc.sync.dma_start(
                out=raw[:], in_=matrix[first : first + tiles * P, columns].rearrange("(t p) k -> p t k", p=P)
            )
            return raw

        def load_dic(c):
            raw = raw_pool.tile([P, PACK, Z_DIM], BF16, tag="raw")
            nc.sync.dma_start(
                out=raw[:], in_=dic[c * K_PASS : (c + 1) * K_PASS, :].rearrange("(p t) d -> p t d", t=PACK)
            )
            return raw

        def load_x(half):
            return load_rows(x, half * HALF_ROWS, HALF_TILES, slice(0, X_DIM))

        def load_w(chunk, half, columns):
            return load_rows(cs_w, chunk * ROWS + half * HALF_ROWS, HALF_TILES, columns)

        dic_raw = [load_dic(0)]
        att_raw = [load_att(pair) for pair in range(2)]
        x_raw = [load_x(0)]
        dic_raw.extend([load_dic(c) for c in range(1, DICT_PASSES)])
        x_raw.append(load_x(1))
        w_raw = {(0, half): load_w(0, half, slice(0, X_DIM)) for half in range(HALVES)}

        identity = const.tile([P, P], F32)
        make_identity(nc, identity[:])

        att_codes = keep.tile([P, DICT_PASSES, TOKENS], U32, align_bytes=64)
        att_scales = keep.tile([P, DICT_PASSES, TOKENS], U8, align_bytes=64)
        dic_codes = moving_pool.tile([P, DICT_PASSES, Z_DIM], U32, tag="codes", align_bytes=64)
        dic_scales = moving_pool.tile([P, DICT_PASSES, Z_DIM], U8, tag="scales", align_bytes=64)
        xz_codes = keep.tile([P, XZ_PASSES, TOKENS], U32, align_bytes=64)
        xz_scales = keep.tile([P, XZ_PASSES, TOKENS], U8, align_bytes=64)
        z_sb = keep.tile([P, ROW_TILES, Z_DIM], F32)

        def empty_bank(on_vector, out, in_):
            if on_vector:
                nc.vector.tensor_copy(out=out, in_=in_)
            else:
                nc.scalar.copy(out=out, in_=in_)

        def new_grouped():
            grouped = grouped_pool.tile([P, PACK * ROWS], BF16, tag="grouped", align_bytes=64)
            return grouped

        def transpose_256_rows(words_of, grouped, part, on_vector):
            bank = transposed.tile([P, 2, 2 * P], F32, tag="bank")
            for u in range(2):
                for i in range(2):
                    nc.tensor.transpose(bank[:, u, i * P : (i + 1) * P], words_of(i, u), identity[:])
            pairs = grouped[:].bitcast(F32).rearrange("p (r u) -> p r u", u=2)
            empty_bank(on_vector, pairs[:, part * 2 * P : (part + 1) * 2 * P, :], bank[:].rearrange("p u r -> p r u"))

        def words_of_rows(raw):
            words = raw[:].rearrange("p t k -> p (t k)").bitcast(F32)
            return words.rearrange("p (t w) -> p t w", t=raw.shape[1])

        def every_second_word(words):
            return lambda g: lambda i, u: words[:, i, g * WORDS + u : (g + 1) * WORDS : 2]

        def split_words(j):
            chunk, r = divmod(j, RUNS_PER_CHUNK)
            split = split_pool.tile([P, ROW_TILES, RUN_PASSES, 2, P], F32, tag="split")
            for t in range(ROW_TILES):
                if j == FIRST_Z_RUN:
                    words = words_of_rows(w_raw_z)[:, t, :]
                else:
                    words = words_of_rows(w_raw[(chunk, t // HALF_TILES)])[:, t % HALF_TILES, :]
                    words = words[:, r * RUN_PASSES * WORDS : (r + 1) * RUN_PASSES * WORDS]
                nc.vector.tensor_copy(
                    out=split[:, t, :, :, :], in_=words.rearrange("p (s m u) -> p s u m", u=2, m=P)
                )
            return split

        def split_half(words):
            split = split_pool.tile([P, HALF_TILES, X_PASSES, 2, P], F32, tag="split")
            src = words[:, :, 0 : X_PASSES * WORDS].rearrange("p t (s m u) -> p t s u m", u=2, m=P)
            nc.scalar.copy(out=split[:, 0, :, :, :], in_=src[:, 0])
            nc.vector.tensor_copy(out=split[:, 1, :, :, :], in_=src[:, 1])
            return lambda g: lambda i, u: split[:, i, g, u, :]

        def transpose_pair(source_of, r, last_on_vector=False):
            grouped = new_grouped()
            for s in range(RUN_PASSES):
                transpose_256_rows(source_of(r * RUN_PASSES + s), grouped, s, last_on_vector and s == RUN_PASSES - 1)
            return grouped

        def quantise_pair(half, r, grouped, codes, scales):
            columns = slice(half * HALF_ROWS, (half + 1) * HALF_ROWS)
            width = PACK * HALF_ROWS
            for s in range(RUN_PASSES):
                nc.vector.quantize_mx(
                    out=codes[:, r * RUN_PASSES + s, columns].bitcast(FP8X4),
                    scales=scales[:, r * RUN_PASSES + s, columns],
                    in_=grouped[:, s * width : (s + 1) * width],
                )

        def quantise(grouped_tiles, codes, scales, first_pass):
            for s, grouped in enumerate(grouped_tiles):
                nc.vector.quantize_mx(
                    out=codes[:, first_pass + s, :].bitcast(FP8X4),
                    scales=scales[:, first_pass + s, :],
                    in_=grouped[:],
                )

        def regroup_dic(piece):
            c, h = divmod(piece, 2)
            grouped = new_grouped()
            dst = grouped[:].rearrange("p (c i t) -> p c t i", i=4, t=PACK)
            src = dic_raw[c][:, :, h * ROWS : (h + 1) * ROWS].rearrange("p t (c i) -> p c t i", i=4)
            middle = ROWS // 4 // 2
            nc.vector.tensor_copy(out=dst[:, 0:middle], in_=src[:, 0:middle])
            nc.scalar.copy(out=dst[:, middle:], in_=src[:, middle:])
            return grouped

        def quantise_dic(piece):
            c, h = divmod(piece, 2)
            columns = slice(h * ROWS, (h + 1) * ROWS)
            nc.vector.quantize_mx(
                out=dic_codes[:, c, columns].bitcast(FP8X4),
                scales=dic_scales[:, c, columns],
                in_=dic_grouped[piece][:],
            )

        z_sums = {}

        def multiply_dic(piece):
            c, h = divmod(piece, 2)
            columns = slice(h * ROWS, (h + 1) * ROWS)
            for t in range(ROW_TILES):
                if c == 0:
                    if h == 0:
                        bank = transposed.tile([P, ROWS], F32, tag="bank")
                    else:
                        bank = sums.tile([P, ROWS], F32, tag="sum")
                    z_sums[(t, h)] = bank
                nc.tensor.matmul_mx(
                    out=z_sums[(t, h)][:],
                    lhsT=att_codes[:, c, t * P : (t + 1) * P].bitcast(FP8X4),
                    lhsT_scale=att_scales[:, c, t * P : (t + 1) * P],
                    rhs=dic_codes[:, c, columns].bitcast(FP8X4),
                    rhs_scale=dic_scales[:, c, columns],
                    start=(c == 0),
                    stop=(c == DICT_PASSES - 1),
                )

        dic_grouped = [regroup_dic(piece) for piece in range(2)]
        for piece in range(2):
            quantise_dic(piece)

        att_grouped = [new_grouped() for c in range(DICT_PASSES)]
        for pair in range(2):
            source_of = every_second_word(words_of_rows(att_raw[pair]))
            for c in range(DICT_PASSES):
                transpose_256_rows(source_of(c), att_grouped[c], pair, c == 0)
        quantise(att_grouped, att_codes, att_scales, 0)

        x_source = every_second_word(words_of_rows(x_raw[0]))
        x_grouped = [transpose_pair(x_source, r) for r in range(X_RUNS)]

        for piece in range(PIECES):
            if piece >= 2:
                quantise_dic(piece)
            multiply_dic(piece)
            if piece + 2 < PIECES:
                dic_grouped.append(regroup_dic(piece + 2))
            if piece < X_RUNS:
                quantise_pair(0, piece, x_grouped[piece], xz_codes, xz_scales)

        w_raw_z = load_rows(cs_w, 0, ROW_TILES, slice(X_DIM, XZ_DIM))
        for half in range(HALVES):
            w_raw[(1, half)] = load_w(1, half, slice(0, XZ_DIM))
        bias = const.tile([P, OUT_DIM], BF16)
        nc.sync.dma_start(out=bias[:], in_=cs_b.partition_broadcast(P))
        for half in range(HALVES):
            w_raw[(2, half)] = load_w(2, half, slice(0, XZ_DIM))

        x_source = split_half(words_of_rows(x_raw[1]))
        for h in range(2):
            for t in range(ROW_TILES):
                empty_bank(t % 2 == 0, z_sb[:, t, h * ROWS : (h + 1) * ROWS], z_sums[(t, h)][:])

        def round_z(s):
            z_words = z_words_pool.tile([P, ROW_TILES, 2, P, 2], BF16, tag="z_words")
            for t in range(ROW_TILES):
                nc.vector.tensor_copy(
                    out=z_words[:, t, :, :, :],
                    in_=z_sb[:, t, s * K_PASS : (s + 1) * K_PASS].rearrange("p (m u e) -> p u m e", u=2, e=2),
                )
            return z_words

        def transpose_z(z_words):
            words = z_words[:].rearrange("p t u m e -> p (t u m e)").bitcast(F32)
            words = words.rearrange("p (t u m) -> p t u m", t=ROW_TILES, u=2)
            grouped = new_grouped()
            for half in range(HALVES):
                own = words[:, half * HALF_TILES : (half + 1) * HALF_TILES]
                transpose_256_rows(lambda i, u: own[:, i, u, :], grouped, half, False)
            return [grouped]

        w_codes, w_scales, logit_sums = [], [], []
        w_source = {}

        def split_w(j):
            if j < W_RUNS:
                w_source[j] = split_words(j)

        def new_chunk():
            codes = moving_pool.tile([P, XZ_PASSES, ROWS], U32, tag="codes", align_bytes=64)
            scales = moving_pool.tile([P, XZ_PASSES, ROWS], U8, tag="scales", align_bytes=64)
            w_codes.append(codes)
            w_scales.append(scales)

        def transpose_w(j):
            grouped_tiles = []
            for s in range(RUN_PASSES):
                grouped = new_grouped()
                for half in range(HALVES):
                    own = w_source[j][:, half * HALF_TILES : (half + 1) * HALF_TILES, s, :, :]
                    transpose_256_rows(lambda i, u: own[:, i, u, :], grouped, half, False)
                grouped_tiles.append(grouped)
            return grouped_tiles

        def quantise_w(j, grouped_tiles):
            chunk, r = divmod(j, RUNS_PER_CHUNK)
            if r == 0:
                new_chunk()
            quantise(grouped_tiles, w_codes[chunk], w_scales[chunk], r * RUN_PASSES)

        def multiply_one(chunk, g, t):
            if g == 0:
                bank = sums.tile([P, ROWS], F32, tag="sum")
                logit_sums.append(bank)
            nc.tensor.matmul_mx(
                out=logit_sums[chunk * ROW_TILES + t][:],
                lhsT=xz_codes[:, g, t * P : (t + 1) * P].bitcast(FP8X4),
                lhsT_scale=xz_scales[:, g, t * P : (t + 1) * P],
                rhs=w_codes[chunk][:, g, :].bitcast(FP8X4),
                rhs_scale=w_scales[chunk][:, g, :],
                start=(g == 0),
                stop=(g == XZ_PASSES - 1),
            )

        def multiply_pass_of_w(j, s):
            chunk, r = divmod(j, RUNS_PER_CHUNK)
            for t in range(ROW_TILES):
                multiply_one(chunk, r * RUN_PASSES + s, t)

        def multiply_w(j):
            chunk, r = divmod(j, RUNS_PER_CHUNK)
            columns = slice(chunk * ROWS, (chunk + 1) * ROWS)
            for t in range(ROW_TILES):
                for g in range(r * RUN_PASSES, (r + 1) * RUN_PASSES):
                    multiply_one(chunk, g, t)
                if r == RUNS_PER_CHUNK - 1:
                    bank = logit_sums[chunk * ROW_TILES + t]
                    result = result_pool.tile([P, ROWS], F32, tag="result")
                    nc.vector.tensor_tensor(
                        out=result[:], in0=bank[:], in1=bias[:, columns], op=mybir.AluOpType.add
                    )
                    nc.sync.dma_start(out=logits_out[t * P : (t + 1) * P, columns], in_=result[:])

        new_chunk()
        w_sources = [every_second_word(words_of_rows(w_raw[(0, half)])) for half in range(HALVES)]

        def prepare_x(r):
            quantise_pair(1, r, transpose_pair(x_source, r, True), xz_codes, xz_scales)

        def prepare_first(half, r):
            quantise_pair(half, r, transpose_pair(w_sources[half], r), w_codes[0], w_scales[0])

        prepare_x(0)
        prepare_first(0, 0)
        prepare_x(1)
        prepare_first(1, 0)
        prepare_first(0, 1)
        split_w(2)
        prepare_first(1, 1)
        multiply_w(0)
        z_words = [round_z(s) for s in range(Z_PASSES)]
        quantise_w(2, transpose_w(2))
        split_w(3)
        multiply_pass_of_w(1, 0)
        z_grouped = [transpose_z(z_words[s]) for s in range(Z_PASSES)]
        for s in range(Z_PASSES):
            quantise(z_grouped[s], xz_codes, xz_scales, X_PASSES + s)
        multiply_pass_of_w(1, 1)
        split_w(4)
        quantise_w(3, transpose_w(3))
        for t in range(ROW_TILES):
            nc.sync.dma_start(out=z_out[t * P : (t + 1) * P, :], in_=z_sb[:, t, :])
        for j in range(2, W_RUNS):
            multiply_w(j)
            split_w(j + 3)
            if j + 2 < W_RUNS:
                quantise_w(j + 2, transpose_w(j + 2))
